import numpy as np
import ml_dtypes


def mxq(x, axis, fmt="e4m3"):
    dtype, down = {"e4m3": (ml_dtypes.float8_e4m3fn, 7), "e5m2": (ml_dtypes.float8_e5m2, 14)}[fmt]
    v = np.moveaxis(np.asarray(x, np.float32).astype(ml_dtypes.bfloat16).astype(np.float64), axis, -1)
    blocks = v.reshape(v.shape[:-1] + (-1, 32))
    amax = np.abs(blocks).max(-1, keepdims=True)
    byte = np.maximum(np.where(amax > 0, np.frexp(amax)[1] - 1 + 127, 0) - down, 1)
    scale = np.exp2(byte - 127.0)
    codes = (blocks / scale).astype(np.float32).astype(dtype).astype(np.float64)
    return np.moveaxis((codes * scale).reshape(v.shape), -1, axis)


BF16 = ml_dtypes.bfloat16


def bf(x):
    return np.asarray(x, np.float32).astype(BF16)


def f64(x):
    return np.asarray(x).astype(np.float64)


B, IN, OUT, ND, R = 1024, 1024, 512, 8, 4


def setup_inputs():
    p = np.random.standard_normal((R, IN)) / np.sqrt(IN)
    a = np.sqrt(2.0 / R)
    x = np.random.standard_normal((B, R)) @ p * a
    centers = (np.random.standard_normal((OUT * ND, R)) @ p * a).reshape(OUT, ND, IN)
    return {"x": bf(x), "centers": bf(centers)}


def reference(x, centers):
    x = f64(x)
    centers = f64(centers)
    O, D, F = centers.shape
    c = centers.reshape(O * D, F)
    x2 = np.sum(x * x, axis=-1, keepdims=True)
    c2 = np.sum(c * c, axis=-1)[None, :]
    d2 = x2 - 2.0 * (mxq(x, 1, "e4m3") @ mxq(c, 1, "e4m3").T) + c2
    sigma = 1.0
    probs = np.exp(-d2 / (2.0 * sigma * sigma)).reshape(-1, O, D)
    out = (np.max(probs, axis=-1) * (D + 1) - np.sum(probs, axis=-1)) / D
    return out

@@ -1,0 +1,274 @@
+import math
+from contextlib import ExitStack
+
+import concourse.mybir as mybir
+from concourse.masks import make_identity
+
+F32 = mybir.dt.float32
+BF16 = mybir.dt.bfloat16
+U32 = mybir.dt.uint32
+U8 = mybir.dt.uint8
+FP8X4 = mybir.dt.float8_e4m3fn_x4
+ALU = mybir.AluOpType
+ACT = mybir.ActivationFunctionType
+
+P = 128
+FEAT = 1024
+WORDS = FEAT // 2
+ND = 8
+HALF_B = 512
+N_STEPS = 64
+AHEAD = 3
+LAG = 2
+
+FLOPS = 2 * 1024 * 4096 * 1024
+
+
+def tile_pnn_kernel(tc, x, centers, out):
+    nc = tc.nc
+    with ExitStack() as ctx:
+        const = ctx.enter_context(tc.tile_pool(name="const", bufs=1))
+        nat = ctx.enter_context(tc.tile_pool(name="nat", bufs=1))
+        keep = ctx.enter_context(tc.tile_pool(name="keep", bufs=1))
+        stage = ctx.enter_context(tc.tile_pool(name="stage", bufs=3))
+        probs = ctx.enter_context(tc.tile_pool(name="probs", bufs=16))
+        small = ctx.enter_context(tc.tile_pool(name="small", bufs=2))
+        ps_g = ctx.enter_context(tc.psum_pool(name="ps_g", bufs=4))
+        ps_t = ctx.enter_context(tc.psum_pool(name="ps_t", bufs=3))
+        ps_r = ctx.enter_context(tc.psum_pool(name="ps_r", bufs=1))
+
+        warm = const.tile([P, 1], F32, name="warm")
+        nc.vector.memset(warm[:], 0.0)
+        nc.scalar.activation(out=warm[:], in_=warm[:], func=ACT.Exp)
+        ident = const.tile([P, P], F32, name="ident")
+        make_identity(nc, ident[:])
+        junk_s = const.tile([P, FEAT], BF16, name="junk_s")
+
+        def new_chunk(kind, a, b):
+            tagname = "%s%d%d" % (kind, a, b)
+            return {
+                "kind": kind,
+                "nat": nat.tile([P, 4 * FEAT], BF16, name="nat_" + tagname),
+                "codes": keep.tile([P, 4 * FEAT // 4], U32, name="codes_" + tagname, align_bytes=64),
+                "scales": keep.tile([P, 4 * FEAT // 4], U8, name="scales_" + tagname, align_bytes=64),
+                "half": keep.tile([P, 4], F32, name="half_" + tagname),
+                "banks": {},
+            }
+
+        xs = [new_chunk("x", bh, 0) for bh in range(2)]
+        cs = [[new_chunk("c", ot, h) for h in range(2)] for ot in range(4)]
+        xb = [keep.tile([P, HALF_B], F32, name="xb%d" % bh) for bh in range(2)]
+
+        def load(chunk, src, pieces):
+            dst = chunk["nat"][:].rearrange("p (t k) -> p t k", t=4)
+            step = 4 // pieces
+            for i in range(pieces):
+                nc.sync.dma_start(out=dst[:, i * step : (i + 1) * step, :], in_=src[:, i * step : (i + 1) * step, :])
+
+        def load_x(bh, pieces):
+            load(xs[bh], x[bh * HALF_B : (bh + 1) * HALF_B, :].rearrange("(p t) k -> p t k", t=4), pieces)
+
+        def load_c(ot, h, pieces):
+            load(cs[ot][h], centers[ot * P : (ot + 1) * P, 4 * h : 4 * h + 4, :], pieces)
+
+        load_x(0, 2)
+        load_c(0, 0, 2)
+        load_c(0, 1, 1)
+        load_x(1, 1)
+        for ot in range(1, 4):
+            for h in range(2):
+                load_c(ot, h, 1)
+
+        def norm(chunk, j):
+            blk = chunk["nat"][:, j * FEAT : (j + 1) * FEAT]
+            nc.scalar.activation(
+                out=junk_s[:], in_=blk, func=ACT.Square, scale=math.sqrt(0.5), accum_out=chunk["half"][:, j : j + 1],
+            )
+
+        def transposes(chunk, j):
+            bank = ps_t.tile([P, WORDS], F32, name="xt")
+            words = chunk["nat"][:].bitcast(F32)
+            for q in range(4):
+                nc.tensor.transpose(
+                    bank[:, q * P : (q + 1) * P],
+                    words[:, j * WORDS + q * P : j * WORDS + (q + 1) * P],
+                    ident[:],
+                )
+            chunk["banks"][j] = bank
+
+        def copy_out(chunk, j, on_scalar):
+            if j == 0:
+                chunk["grouped"] = stage.tile([P, 4 * FEAT], BF16, name="grouped", align_bytes=64)
+            gw = chunk["grouped"][:].bitcast(F32)
+            src = chunk["banks"][j][:].rearrange("p (g u r) -> p g r u", g=2, u=2)
+            if chunk["kind"] == "c":
+                dst = gw[:, j * WORDS : (j + 1) * WORDS].rearrange("p (g r u) -> p g r u", g=2, u=2)
+            else:
+                dst = gw.rearrange("p (g c u) -> p g c u", g=2, u=2)[:, :, j * P : (j + 1) * P, :]
+            if on_scalar:
+                nc.scalar.copy(out=dst, in_=src)
+            else:
+                nc.vector.tensor_copy(out=dst, in_=src)
+
+        def quantise(chunk):
+            nc.vector.quantize_mx(out=chunk["codes"][:].bitcast(FP8X4), scales=chunk["scales"][:], in_=chunk["grouped"][:])
+
+        def spread_x_norm(bh):
+            bank = ps_r.tile([P, HALF_B], F32, name="xrow", tag="r")
+            for t in range(4):
+                nc.tensor.matmul(
+                    out=bank[:, t * P : (t + 1) * P],
+                    lhsT=xs[bh]["half"][:, t : t + 1].to_broadcast([P, P]),
+                    rhs=ident[:], start=True, stop=True,
+                )
+            nc.scalar.copy(out=xb[bh][:], in_=bank[:])
+
+        def prepare_at_once(chunk):
+            for j in range(4):
+                transposes(chunk, j)
+                norm(chunk, j)
+                copy_out(chunk, j, False)
+            quantise(chunk)
+
+        g_banks = {}
+        e_tiles = {}
+        naccs = {}
+
+        def mx(s):
+            n, d = divmod(s, ND)
+            ot, bh = divmod(n, 2)
+            c = cs[ot][d // 4]
+            bank = ps_g.tile([P, HALF_B], F32, name="g")
+            for g in range(2):
+                w = slice((d % 4) * 2 * P + g * P, (d % 4) * 2 * P + (g + 1) * P)
+                m = slice(g * HALF_B, (g + 1) * HALF_B)
+                nc.tensor.matmul_mx(
+                    out=bank[:],
+                    lhsT=c["codes"][:, w].bitcast(FP8X4), lhsT_scale=c["scales"][:, w],
+                    rhs=xs[bh]["codes"][:, m].bitcast(FP8X4), rhs_scale=xs[bh]["scales"][:, m],
+                    start=(g == 0), stop=(g == 1),
+                )
+            g_banks[s] = bank
+
+        def exponent_and_exp(s):
+            n, d = divmod(s, ND)
+            ot, bh = divmod(n, 2)
+            e = probs.tile([P, HALF_B], F32, name="e")
+            nc.vector.scalar_tensor_tensor(
+                out=e[:], in0=g_banks[s][:], scalar=cs[ot][d // 4]["half"][:, d % 4 : d % 4 + 1],
+                in1=xb[bh][:], op0=ALU.subtract, op1=ALU.subtract,
+            )
+            nc.scalar.activation(out=e[:], in_=e[:], func=ACT.Exp)
+            e_tiles[s] = e
+
+        def running_min(s):
+            n, d = divmod(s, ND)
+            if d == 0:
+                naccs[n] = small.tile([P, HALF_B], F32, name="nacc")
+                nc.vector.tensor_scalar(out=naccs[n][:], in0=e_tiles[s][:], scalar1=-9.0, scalar2=None, op0=ALU.mult)
+            else:
+                nc.vector.scalar_tensor_tensor(
+                    out=naccs[n][:], in0=e_tiles[s][:], scalar=-9.0, in1=naccs[n][:], op0=ALU.mult, op1=ALU.min,
+                )
+
+        r_banks = {}
+
+        def add_up_transposed(n):
+            bank = ps_r.tile([P, HALF_B], F32, name="r", tag="r")
+            terms = [e_tiles[n * ND + d] for d in range(ND)] + [naccs[n]]
+            for t in range(4):
+                for i, term in enumerate(terms):
+                    nc.tensor.matmul(
+                        out=bank[:, t * P : (t + 1) * P], lhsT=term[:, t * P : (t + 1) * P], rhs=ident[:],
+                        start=(i == 0), stop=(i == len(terms) - 1), is_transpose=True,
+                    )
+            r_banks[n] = bank
+
+        def store(n, res):
+            ot, bh = divmod(n, 2)
+            nc.sync.dma_start(
+                out=out[bh * HALF_B : (bh + 1) * HALF_B, ot * P : (ot + 1) * P].rearrange("(p t) o -> p t o", t=4),
+                in_=res[:].rearrange("p (t o) -> p t o", t=4),
+            )
+
+        def finish(n):
+            res = small.tile([P, HALF_B], F32, name="res")
+            nc.scalar.mul(out=res[:], in_=r_banks[n][:], mul=-0.125)
+            store(n, res)
+
+        last_banks = []
+        waiting = []
+        served = {"n": 0}
+
+        def add_term(t, term, first, last):
+            nc.tensor.matmul(
+                out=last_banks[t][:, 0:P], lhsT=term[:, t * P : (t + 1) * P], rhs=ident[:],
+                start=first, stop=last, is_transpose=True,
+            )
+
+        def add_last(term, first, last, fourth_free):
+            if first:
+                for t in range(3):
+                    last_banks.append(ps_t.tile([P, WORDS], F32, name="xt"))
+            for t in range(3):
+                add_term(t, term, first, last)
+            waiting.append((term, first, last))
+            if fourth_free:
+                if len(last_banks) == 3:
+                    last_banks.append(ps_r.tile([P, HALF_B], F32, name="r", tag="r"))
+                for w in waiting[served["n"] :]:
+                    add_term(3, w[0], w[1], w[2])
+                served["n"] = len(waiting)
+
+        def finish_last(n):
+            res = small.tile([P, HALF_B], F32, name="res")
+            for t in range(4):
+                dst = res[:, t * P : (t + 1) * P]
+                if t % 2 == 0:
+                    nc.scalar.mul(out=dst, in_=last_banks[t][:, 0:P], mul=-0.125)
+                else:
+                    nc.vector.tensor_scalar(out=dst, in0=last_banks[t][:, 0:P], scalar1=-0.125, scalar2=None, op0=ALU.mult)
+            store(n, res)
+
+        LAST = N_STEPS // ND - 1
+        prepare_at_once(xs[0])
+        spread_x_norm(0)
+        prepare_at_once(cs[0][0])
+        for s in range(AHEAD):
+            mx(s)
+        for s in range(N_STEPS + LAG + 1):
+            if s + AHEAD < N_STEPS:
+                if s + AHEAD == 4:
+                    prepare_at_once(cs[0][1])
+                if s + AHEAD == ND:
+                    prepare_at_once(xs[1])
+                    spread_x_norm(1)
+                mx(s + AHEAD)
+            if s % ND == LAG and ND <= s < N_STEPS:
+                add_up_transposed(s // ND - 1)
+            nxt, l = divmod(s, 2 * ND)
+            nxt += 1
+            prep = nxt < 4
+            if prep and l % 4 == 2:
+                for j in (l // 2 - 1, l // 2):
+                    transposes(cs[nxt][j // 4], j % 4)
+            if s < N_STEPS:
+                exponent_and_exp(s)
+                if s // ND == LAST:
+                    add_last(e_tiles[s], s % ND == 0, False, s % ND > 5)
+            if 0 <= s - LAG < N_STEPS:
+                running_min(s - LAG)
+            if prep and l % 2 == 0:
+                norm(cs[nxt][l // 8], (l // 2) % 4)
+            if prep and l % 4 == 3:
+                j = (l - 3) // 2
+                copy_out(cs[nxt][j // 4], j % 4, True)
+                copy_out(cs[nxt][j // 4], j % 4 + 1, False)
+            if prep and l == 9:
+                quantise(cs[nxt][0])
+            if 1 <= nxt - 1 < 4 and l == 0:
+                quantise(cs[nxt - 1][1])
+            if s % ND == 5 and ND <= s < N_STEPS:
+                finish(s // ND - 1)
+        add_last(naccs[LAST], False, True, True)
+        finish_last(LAST)

@@ -15,10 +15,13 @@ ACT = mybir.ActivationFunctionType
 P = 128
 FEAT = 1024
 WORDS = FEAT // 2
+B = 1024
 ND = 8
+TILES = 4
 HALF_B = 512
-N_STEPS = 64
-AHEAD = 3
+STEPS = TILES * ND
+LAST = TILES - 1
+AHEAD = 2
 LAG = 2
 
 FLOPS = 2 * 1024 * 4096 * 1024
@@ -28,10 +31,10 @@ def tile_pnn_kernel(tc, x, centers, out):
     nc = tc.nc
     with ExitStack() as ctx:
         const = ctx.enter_context(tc.tile_pool(name="const", bufs=1))
-        nat = ctx.enter_context(tc.tile_pool(name="nat", bufs=1))
+        nat = ctx.enter_context(tc.tile_pool(name="nat", bufs=8))
         keep = ctx.enter_context(tc.tile_pool(name="keep", bufs=1))
         stage = ctx.enter_context(tc.tile_pool(name="stage", bufs=3))
-        probs = ctx.enter_context(tc.tile_pool(name="probs", bufs=16))
+        probs = ctx.enter_context(tc.tile_pool(name="probs", bufs=18))
         small = ctx.enter_context(tc.tile_pool(name="small", bufs=2))
         ps_g = ctx.enter_context(tc.psum_pool(name="ps_g", bufs=4))
         ps_t = ctx.enter_context(tc.psum_pool(name="ps_t", bufs=3))
@@ -43,21 +46,19 @@ def tile_pnn_kernel(tc, x, centers, out):
         ident = const.tile([P, P], F32, name="ident")
         make_identity(nc, ident[:])
         junk_s = const.tile([P, FEAT], BF16, name="junk_s")
+        xb = const.tile([P, B], F32, name="xb")
 
         def new_chunk(kind, a, b):
             tagname = "%s%d%d" % (kind, a, b)
             return {
                 "kind": kind,
-                "nat": nat.tile([P, 4 * FEAT], BF16, name="nat_" + tagname),
+                "nat": nat.tile([P, 4 * FEAT], BF16, name="nat_" + tagname, tag="nat"),
                 "codes": keep.tile([P, 4 * FEAT // 4], U32, name="codes_" + tagname, align_bytes=64),
                 "scales": keep.tile([P, 4 * FEAT // 4], U8, name="scales_" + tagname, align_bytes=64),
                 "half": keep.tile([P, 4], F32, name="half_" + tagname),
+                "neg": keep.tile([P, 4], F32, name="neg_" + tagname),
                 "banks": {},
             }
-
-        xs = [new_chunk("x", bh, 0) for bh in range(2)]
-        cs = [[new_chunk("c", ot, h) for h in range(2)] for ot in range(4)]
-        xb = [keep.tile([P, HALF_B], F32, name="xb%d" % bh) for bh in range(2)]
 
         def load(chunk, src, pieces):
             dst = chunk["nat"][:].rearrange("p (t k) -> p t k", t=4)
@@ -65,17 +66,20 @@ def tile_pnn_kernel(tc, x, centers, out):
             for i in range(pieces):
                 nc.sync.dma_start(out=dst[:, i * step : (i + 1) * step, :], in_=src[:, i * step : (i + 1) * step, :])
 
+        xs = {}
+        cs = {}
+
         def load_x(bh, pieces):
+            xs[bh] = new_chunk("x", bh, 0)
             load(xs[bh], x[bh * HALF_B : (bh + 1) * HALF_B, :].rearrange("(p t) k -> p t k", t=4), pieces)
 
         def load_c(ot, h, pieces):
-            load(cs[ot][h], centers[ot * P : (ot + 1) * P, 4 * h : 4 * h + 4, :], pieces)
+            cs[(ot, h)] = new_chunk("c", ot, h)
+            load(cs[(ot, h)], centers[ot * P : (ot + 1) * P, 4 * h : 4 * h + 4, :], pieces)
 
-        load_x(0, 2)
-        load_c(0, 0, 2)
-        load_c(0, 1, 1)
-        load_x(1, 1)
-        for ot in range(1, 4):
+        load_x(0, 4)
+        load_x(1, 2)
+        for ot in range(TILES):
             for h in range(2):
                 load_c(ot, h, 1)
 
@@ -83,6 +87,16 @@ def tile_pnn_kernel(tc, x, centers, out):
             blk = chunk["nat"][:, j * FEAT : (j + 1) * FEAT]
             nc.scalar.activation(
                 out=junk_s[:], in_=blk, func=ACT.Square, scale=math.sqrt(0.5), accum_out=chunk["half"][:, j : j + 1],
+            )
+
+        def norm_c(s):
+            ot, d = divmod(s, ND)
+            chunk = cs[(ot, d // 4)]
+            j = d % 4
+            norm(chunk, j)
+            nc.gpsimd.tensor_scalar(
+                out=chunk["neg"][:, j : j + 1], in0=chunk["half"][:, j : j + 1], scalar1=-1.0, scalar2=0.0,
+                op0=ALU.mult, op1=ALU.add,
             )
 
         def transposes(chunk, j):
@@ -110,8 +124,12 @@ def tile_pnn_kernel(tc, x, centers, out):
             else:
                 nc.vector.tensor_copy(out=dst, in_=src)
 
-        def quantise(chunk):
-            nc.vector.quantize_mx(out=chunk["codes"][:].bitcast(FP8X4), scales=chunk["scales"][:], in_=chunk["grouped"][:])
+        def quantise(chunk, part=0, parts=1):
+            w = slice(part * FEAT // parts, (part + 1) * FEAT // parts)
+            nc.vector.quantize_mx(
+                out=chunk["codes"][:, w].bitcast(FP8X4), scales=chunk["scales"][:, w],
+                in_=chunk["grouped"][:, 4 * w.start : 4 * w.stop],
+            )
 
         def spread_x_norm(bh):
             bank = ps_r.tile([P, HALF_B], F32, name="xrow", tag="r")
@@ -121,154 +139,204 @@ def tile_pnn_kernel(tc, x, centers, out):
                     lhsT=xs[bh]["half"][:, t : t + 1].to_broadcast([P, P]),
                     rhs=ident[:], start=True, stop=True,
                 )
-            nc.scalar.copy(out=xb[bh][:], in_=bank[:])
+            xs[bh]["row"] = bank
 
-        def prepare_at_once(chunk):
-            for j in range(4):
-                transposes(chunk, j)
-                norm(chunk, j)
-                copy_out(chunk, j, False)
-            quantise(chunk)
+        def copy_x_norm(bh):
+            nc.scalar.copy(out=xb[:, bh * HALF_B : (bh + 1) * HALF_B], in_=xs[bh]["row"][:])
 
         g_banks = {}
         e_tiles = {}
         naccs = {}
 
         def mx(s):
-            n, d = divmod(s, ND)
-            ot, bh = divmod(n, 2)
-            c = cs[ot][d // 4]
-            bank = ps_g.tile([P, HALF_B], F32, name="g")
-            for g in range(2):
-                w = slice((d % 4) * 2 * P + g * P, (d % 4) * 2 * P + (g + 1) * P)
-                m = slice(g * HALF_B, (g + 1) * HALF_B)
-                nc.tensor.matmul_mx(
-                    out=bank[:],
-                    lhsT=c["codes"][:, w].bitcast(FP8X4), lhsT_scale=c["scales"][:, w],
-                    rhs=xs[bh]["codes"][:, m].bitcast(FP8X4), rhs_scale=xs[bh]["scales"][:, m],
-                    start=(g == 0), stop=(g == 1),
-                )
-            g_banks[s] = bank
+            ot, d = divmod(s, ND)
+            c = cs[(ot, d // 4)]
+            for bh in range(2):
+                bank = ps_g.tile([P, HALF_B], F32, name="g")
+                for g in range(2):
+                    w = slice((d % 4) * 2 * P + g * P, (d % 4) * 2 * P + (g + 1) * P)
+                    m = slice(g * HALF_B, (g + 1) * HALF_B)
+                    nc.tensor.matmul_mx(
+                        out=bank[:],
+                        lhsT=c["codes"][:, w].bitcast(FP8X4), lhsT_scale=c["scales"][:, w],
+                        rhs=xs[bh]["codes"][:, m].bitcast(FP8X4), rhs_scale=xs[bh]["scales"][:, m],
+                        start=(g == 0), stop=(g == 1),
+                    )
+                g_banks[(s, bh)] = bank
 
-        def exponent_and_exp(s):
-            n, d = divmod(s, ND)
-            ot, bh = divmod(n, 2)
-            e = probs.tile([P, HALF_B], F32, name="e")
-            nc.vector.scalar_tensor_tensor(
-                out=e[:], in0=g_banks[s][:], scalar=cs[ot][d // 4]["half"][:, d % 4 : d % 4 + 1],
-                in1=xb[bh][:], op0=ALU.subtract, op1=ALU.subtract,
-            )
-            nc.scalar.activation(out=e[:], in_=e[:], func=ACT.Exp)
+        def minus_x_norm(s):
+            e = probs.tile([P, B], F32, name="e")
+            for bh in range(2):
+                w = slice(bh * HALF_B, (bh + 1) * HALF_B)
+                nc.vector.tensor_tensor(out=e[:, w], in0=g_banks[(s, bh)][:], in1=xb[:, w], op=ALU.subtract)
             e_tiles[s] = e
 
-        def running_min(s):
+        def exponential(s, widths):
+            ot, d = divmod(s, ND)
+            e = e_tiles[s]
+            for i in range(widths):
+                w = slice(i * B // widths, (i + 1) * B // widths)
+                nc.scalar.activation(
+                    out=e[:, w], in_=e[:, w], func=ACT.Exp, bias=cs[(ot, d // 4)]["neg"][:, d % 4 : d % 4 + 1],
+                )
+
+        def running_min(s, widths):
             n, d = divmod(s, ND)
             if d == 0:
-                naccs[n] = small.tile([P, HALF_B], F32, name="nacc")
-                nc.vector.tensor_scalar(out=naccs[n][:], in0=e_tiles[s][:], scalar1=-9.0, scalar2=None, op0=ALU.mult)
-            else:
-                nc.vector.scalar_tensor_tensor(
-                    out=naccs[n][:], in0=e_tiles[s][:], scalar=-9.0, in1=naccs[n][:], op0=ALU.mult, op1=ALU.min,
-                )
+                naccs[n] = small.tile([P, B], F32, name="nacc")
+            for i in range(widths):
+                w = slice(i * B // widths, (i + 1) * B // widths)
+                if d == 0:
+                    nc.vector.tensor_scalar(out=naccs[n][:, w], in0=e_tiles[s][:, w], scalar1=-9.0, scalar2=None, op0=ALU.mult)
+                else:
+                    nc.vector.scalar_tensor_tensor(
+                        out=naccs[n][:, w], in0=e_tiles[s][:, w], scalar=-9.0, in1=naccs[n][:, w], op0=ALU.mult, op1=ALU.min,
+                    )
+
+        def turn(bank_cols, term, cols, first, last):
+            nc.tensor.matmul(out=bank_cols, lhsT=term[:, cols], rhs=ident[:], start=first, stop=last, is_transpose=True)
 
         r_banks = {}
 
-        def add_up_transposed(n):
-            bank = ps_r.tile([P, HALF_B], F32, name="r", tag="r")
+        def add_up(n, bh, blocks):
+            if blocks[0] == 0:
+                r_banks[(n, bh)] = ps_r.tile([P, HALF_B], F32, name="r", tag="r")
             terms = [e_tiles[n * ND + d] for d in range(ND)] + [naccs[n]]
-            for t in range(4):
+            for t in blocks:
                 for i, term in enumerate(terms):
-                    nc.tensor.matmul(
-                        out=bank[:, t * P : (t + 1) * P], lhsT=term[:, t * P : (t + 1) * P], rhs=ident[:],
-                        start=(i == 0), stop=(i == len(terms) - 1), is_transpose=True,
+                    turn(
+                        r_banks[(n, bh)][:, t * P : (t + 1) * P], term, slice(bh * HALF_B + t * P, bh * HALF_B + (t + 1) * P),
+                        i == 0, i == len(terms) - 1,
                     )
-            r_banks[n] = bank
 
-        def store(n, res):
-            ot, bh = divmod(n, 2)
+        def store(n, bh, res):
             nc.sync.dma_start(
-                out=out[bh * HALF_B : (bh + 1) * HALF_B, ot * P : (ot + 1) * P].rearrange("(p t) o -> p t o", t=4),
+                out=out[bh * HALF_B : (bh + 1) * HALF_B, n * P : (n + 1) * P].rearrange("(p t) o -> p t o", t=4),
                 in_=res[:].rearrange("p (t o) -> p t o", t=4),
             )
 
-        def finish(n):
+        def finish(n, bh):
             res = small.tile([P, HALF_B], F32, name="res")
-            nc.scalar.mul(out=res[:], in_=r_banks[n][:], mul=-0.125)
-            store(n, res)
+            nc.scalar.mul(out=res[:], in_=r_banks[(n, bh)][:], mul=-0.125)
+            store(n, bh, res)
 
-        last_banks = []
-        waiting = []
-        served = {"n": 0}
+        last_banks = {}
 
-        def add_term(t, term, first, last):
-            nc.tensor.matmul(
-                out=last_banks[t][:, 0:P], lhsT=term[:, t * P : (t + 1) * P], rhs=ident[:],
-                start=first, stop=last, is_transpose=True,
-            )
+        def last_terms(bh, blocks, ds, with_max):
+            for t in blocks:
+                if (bh, t) not in last_banks:
+                    if bh == 0 and t < 3:
+                        last_banks[(bh, t)] = ps_t.tile([P, WORDS], F32, name="xt")
+                    elif bh == 0:
+                        last_banks[(bh, t)] = ps_r.tile([P, HALF_B], F32, name="r", tag="r")
+                    else:
+                        last_banks[(bh, t)] = ps_g.tile([P, HALF_B], F32, name="g")
+            for i in list(ds) + ([ND] if with_max else []):
+                for t in blocks:
+                    term = naccs[LAST] if i == ND else e_tiles[LAST * ND + i]
+                    turn(
+                        last_banks[(bh, t)][:, 0:P], term, slice(bh * HALF_B + t * P, bh * HALF_B + (t + 1) * P),
+                        i == 0, i == ND,
+                    )
 
-        def add_last(term, first, last, fourth_free):
-            if first:
-                for t in range(3):
-                    last_banks.append(ps_t.tile([P, WORDS], F32, name="xt"))
-            for t in range(3):
-                add_term(t, term, first, last)
-            waiting.append((term, first, last))
-            if fourth_free:
-                if len(last_banks) == 3:
-                    last_banks.append(ps_r.tile([P, HALF_B], F32, name="r", tag="r"))
-                for w in waiting[served["n"] :]:
-                    add_term(3, w[0], w[1], w[2])
-                served["n"] = len(waiting)
-
-        def finish_last(n):
+        def finish_last(bh):
             res = small.tile([P, HALF_B], F32, name="res")
             for t in range(4):
                 dst = res[:, t * P : (t + 1) * P]
                 if t % 2 == 0:
-                    nc.scalar.mul(out=dst, in_=last_banks[t][:, 0:P], mul=-0.125)
+                    nc.scalar.mul(out=dst, in_=last_banks[(bh, t)][:, 0:P], mul=-0.125)
                 else:
-                    nc.vector.tensor_scalar(out=dst, in0=last_banks[t][:, 0:P], scalar1=-0.125, scalar2=None, op0=ALU.mult)
-            store(n, res)
+                    nc.vector.tensor_scalar(out=dst, in0=last_banks[(bh, t)][:, 0:P], scalar1=-0.125, scalar2=None, op0=ALU.mult)
+            store(LAST, bh, res)
 
-        LAST = N_STEPS // ND - 1
-        prepare_at_once(xs[0])
+        ctx.enter_context(tc.manual_schedule(engines={mybir.EngineType.PE, mybir.EngineType.DVE, mybir.EngineType.Activation}))
+        c0 = cs[(0, 0)]
+
+        for j in range(4):
+            transposes(xs[0], j)
+            norm(xs[0], j)
+            copy_out(xs[0], j, False)
+        for j in range(4):
+            transposes(xs[1], j)
+            norm(xs[1], j)
+            copy_out(xs[1], j, False)
+            if j == 0:
+                quantise(xs[0])
+        transposes(c0, 0)
+        copy_out(c0, 0, False)
+        quantise(xs[1])
+        for j in (1, 2):
+            transposes(c0, j)
+            copy_out(c0, j, False)
+        quantise(c0, 0, 2)
         spread_x_norm(0)
-        prepare_at_once(cs[0][0])
+        copy_x_norm(0)
+        transposes(c0, 3)
+        spread_x_norm(1)
+        norm_c(0)
+        copy_x_norm(1)
+        norm_c(1)
+        copy_out(c0, 3, False)
         for s in range(AHEAD):
             mx(s)
-        for s in range(N_STEPS + LAG + 1):
-            if s + AHEAD < N_STEPS:
-                if s + AHEAD == 4:
-                    prepare_at_once(cs[0][1])
-                if s + AHEAD == ND:
-                    prepare_at_once(xs[1])
-                    spread_x_norm(1)
+        quantise(c0, 1, 2)
+
+        chunks = [cs[(k // 2, k % 2)] for k in range(2 * TILES)]
+        runs = [(chunks[k], j) for k in range(1, 2 * TILES) for j in (0, 2)]
+        turned_at = {r - 1 if r < 2 else 2 * r - 3: r for r in range(len(runs))}
+        second_at = {r if r < 2 else 2 * r - 1: r for r in range(len(runs))}
+
+        def turn_run(r):
+            for j in range(2):
+                transposes(runs[r][0], runs[r][1] + j)
+
+        adds = {}
+        finishes = {}
+        for n in range(LAST):
+            at = (2, 4, 6, 8) if n < LAST - 1 else (2, 3, 5, 6)
+            for i in range(4):
+                adds[(n + 1) * ND + at[i]] = (n, i // 2, (0, 1) if i % 2 == 0 else (2, 3))
+            finishes[(n + 1) * ND + at[1] + 1] = (n, 0)
+            finishes[(n + 1) * ND + at[3] + 1] = (n, 1)
+
+        turn_run(0)
+        for s in range(STEPS + LAG):
+            n, d = divmod(s, ND)
+            new_chunk_due = s < STEPS - AHEAD and s % 4 == 2
+            if new_chunk_due and s > 2:
+                quantise(chunks[(s + AHEAD) // 4])
+            if s < STEPS:
+                minus_x_norm(s)
+            if new_chunk_due and s == 2:
+                quantise(chunks[1])
+            if s + AHEAD < STEPS:
                 mx(s + AHEAD)
-            if s % ND == LAG and ND <= s < N_STEPS:
-                add_up_transposed(s // ND - 1)
-            nxt, l = divmod(s, 2 * ND)
-            nxt += 1
-            prep = nxt < 4
-            if prep and l % 4 == 2:
-                for j in (l // 2 - 1, l // 2):
-                    transposes(cs[nxt][j // 4], j % 4)
-            if s < N_STEPS:
-                exponent_and_exp(s)
-                if s // ND == LAST:
-                    add_last(e_tiles[s], s % ND == 0, False, s % ND > 5)
-            if 0 <= s - LAG < N_STEPS:
-                running_min(s - LAG)
-            if prep and l % 2 == 0:
-                norm(cs[nxt][l // 8], (l // 2) % 4)
-            if prep and l % 4 == 3:
-                j = (l - 3) // 2
-                copy_out(cs[nxt][j // 4], j % 4, True)
-                copy_out(cs[nxt][j // 4], j % 4 + 1, False)
-            if prep and l == 9:
-                quantise(cs[nxt][0])
-            if 1 <= nxt - 1 < 4 and l == 0:
-                quantise(cs[nxt - 1][1])
-            if s % ND == 5 and ND <= s < N_STEPS:
-                finish(s // ND - 1)
-        add_last(naccs[LAST], False, True, True)
-        finish_last(LAST)
+            if s in turned_at:
+                turn_run(turned_at[s])
+            if s < STEPS:
+                exponential(s, 1 if s < STEPS - 1 else 2)
+            if s - 1 in turned_at:
+                copy_out(runs[turned_at[s - 1]][0], runs[turned_at[s - 1]][1], True)
+            if s in second_at:
+                copy_out(runs[second_at[s]][0], runs[second_at[s]][1] + 1, False)
+            if s in finishes:
+                finish(finishes[s][0], finishes[s][1])
+            if s + AHEAD < STEPS:
+                norm_c(s + AHEAD)
+            if s >= LAG:
+                running_min(s - LAG, 1 if s < STEPS + 1 else 2)
+            if s in adds:
+                add_up(adds[s][0], adds[s][1], adds[s][2])
+            if n == LAST and d >= 2:
+                last_terms(0, (0, 1, 2), (d - 2,), False)
+                if d == 7:
+                    last_terms(1, (0, 1), range(0, 6), False)
+            if s == STEPS:
+                last_terms(0, (3,), range(0, 6), False)
+                last_terms(1, (2, 3), range(0, 6), False)
+                for bh in range(2):
+                    last_terms(bh, range(4), (6,), False)
+        for bh in range(2):
+            last_terms(bh, range(4), (7,), True)
+        finish_last(0)
+        finish_last(1)

@@ -46,6 +46,7 @@ def tile_pnn_kernel(tc, x, centers, out):
         ident = const.tile([P, P], F32, name="ident")
         make_identity(nc, ident[:])
         junk_s = const.tile([P, FEAT], BF16, name="junk_s")
+        junk_v = const.tile([P, P], F32, name="junk_v")
         xb = const.tile([P, B], F32, name="xb")
 
         def new_chunk(kind, a, b):
@@ -57,6 +58,7 @@ def tile_pnn_kernel(tc, x, centers, out):
                 "scales": keep.tile([P, 4 * FEAT // 4], U8, name="scales_" + tagname, align_bytes=64),
                 "half": keep.tile([P, 4], F32, name="half_" + tagname),
                 "neg": keep.tile([P, 4], F32, name="neg_" + tagname),
+                "neg_v": keep.tile([P, 4], F32, name="negv_" + tagname),
                 "banks": {},
             }
 
@@ -87,6 +89,27 @@ def tile_pnn_kernel(tc, x, centers, out):
             blk = chunk["nat"][:, j * FEAT : (j + 1) * FEAT]
             nc.scalar.activation(
                 out=junk_s[:], in_=blk, func=ACT.Square, scale=math.sqrt(0.5), accum_out=chunk["half"][:, j : j + 1],
+            )
+
+        def by_gram(s):
+            return 6 <= s < 14
+
+        grams = {}
+
+        def gram(s, bank):
+            chunk = cs[(s // ND, s % ND // 4)]
+            out_cols = bank[:, s % 4 * P : (s % 4 + 1) * P]
+            rows = chunk["grouped"][:, (s % 4) * FEAT : (s % 4 + 1) * FEAT].rearrange("p (g r k) -> p g k r", g=2, k=4)
+            for i in range(8):
+                v = rows[:, i // 4, i % 4, :]
+                nc.tensor.matmul(out=out_cols, lhsT=v, rhs=v, start=(i == 0), stop=(i == 7))
+            grams[s] = out_cols
+
+        def diagonal(s):
+            chunk = cs[(s // ND, s % ND // 4)]
+            nc.vector.scalar_tensor_tensor(
+                out=junk_v[:], in0=grams[s], scalar=-0.5, in1=ident[:], op0=ALU.mult, op1=ALU.mult,
+                accum_out=chunk["neg_v"][:, s % 4 : s % 4 + 1],
             )
 
         def norm_c(s):
@@ -177,21 +200,22 @@ def tile_pnn_kernel(tc, x, centers, out):
             for i in range(widths):
                 w = slice(i * B // widths, (i + 1) * B // widths)
                 nc.scalar.activation(
-                    out=e[:, w], in_=e[:, w], func=ACT.Exp, bias=cs[(ot, d // 4)]["neg"][:, d % 4 : d % 4 + 1],
+                    out=e[:, w], in_=e[:, w], func=ACT.Exp, bias=cs[(ot, d // 4)]["neg_v" if by_gram(s) else "neg"][:, d % 4 : d % 4 + 1],
                 )
 
         def running_min(s, widths):
             n, d = divmod(s, ND)
-            if d == 0:
-                naccs[n] = small.tile([P, B], F32, name="nacc")
             for i in range(widths):
                 w = slice(i * B // widths, (i + 1) * B // widths)
-                if d == 0:
-                    nc.vector.tensor_scalar(out=naccs[n][:, w], in0=e_tiles[s][:, w], scalar1=-9.0, scalar2=None, op0=ALU.mult)
-                else:
-                    nc.vector.scalar_tensor_tensor(
-                        out=naccs[n][:, w], in0=e_tiles[s][:, w], scalar=-9.0, in1=naccs[n][:, w], op0=ALU.mult, op1=ALU.min,
-                    )
+                nc.vector.scalar_tensor_tensor(
+                    out=naccs[n][:, w], in0=e_tiles[s][:, w], scalar=-9.0, in1=naccs[n][:, w], op0=ALU.mult, op1=ALU.min,
+                )
+
+        def first_min(n):
+            naccs[n] = small.tile([P, B], F32, name="nacc")
+            nc.gpsimd.tensor_scalar(
+                out=naccs[n][:], in0=e_tiles[n * ND][:], scalar1=-9.0, scalar2=0.0, op0=ALU.mult, op1=ALU.add,
+            )
 
         def turn(bank_cols, term, cols, first, last):
             nc.tensor.matmul(out=bank_cols, lhsT=term[:, cols], rhs=ident[:], start=first, stop=last, is_transpose=True)
@@ -252,6 +276,7 @@ def tile_pnn_kernel(tc, x, centers, out):
         ctx.enter_context(tc.manual_schedule(engines={mybir.EngineType.PE, mybir.EngineType.DVE, mybir.EngineType.Activation}))
         c0 = cs[(0, 0)]
 
+        c1 = cs[(0, 1)]
         for j in range(4):
             transposes(xs[0], j)
             norm(xs[0], j)
@@ -262,29 +287,33 @@ def tile_pnn_kernel(tc, x, centers, out):
             copy_out(xs[1], j, False)
             if j == 0:
                 quantise(xs[0])
-        transposes(c0, 0)
-        copy_out(c0, 0, False)
-        quantise(xs[1])
-        for j in (1, 2):
+            if j == 2:
+                spread_x_norm(0)
+                copy_x_norm(0)
+        for j in range(2):
             transposes(c0, j)
             copy_out(c0, j, False)
+        quantise(xs[1])
         quantise(c0, 0, 2)
-        spread_x_norm(0)
-        copy_x_norm(0)
-        transposes(c0, 3)
+        for j in range(2, 4):
+            transposes(c0, j)
+            copy_out(c0, j, False)
+        transposes(c1, 0)
         spread_x_norm(1)
         norm_c(0)
         copy_x_norm(1)
-        norm_c(1)
-        copy_out(c0, 3, False)
-        for s in range(AHEAD):
-            mx(s)
+        copy_out(c1, 0, True)
+        mx(0)
+        transposes(c1, 1)
+        copy_out(c1, 1, True)
+        mx(1)
         quantise(c0, 1, 2)
+        transposes(c1, 2)
+        transposes(c1, 3)
 
         chunks = [cs[(k // 2, k % 2)] for k in range(2 * TILES)]
-        runs = [(chunks[k], j) for k in range(1, 2 * TILES) for j in (0, 2)]
-        turned_at = {r - 1 if r < 2 else 2 * r - 3: r for r in range(len(runs))}
-        second_at = {r if r < 2 else 2 * r - 1: r for r in range(len(runs))}
+        runs = [(chunks[k], j) for k in range(2, 2 * TILES) for j in (0, 2)]
+        turned_at = {2 * r + 1: r for r in range(len(runs))}
 
         def turn_run(r):
             for j in range(2):
@@ -293,38 +322,61 @@ def tile_pnn_kernel(tc, x, centers, out):
         adds = {}
         finishes = {}
         for n in range(LAST):
-            at = (2, 4, 6, 8) if n < LAST - 1 else (2, 3, 5, 6)
+            at = (2, 3, 5, 7) if n < LAST - 1 else (2, 3, 5, 6)
             for i in range(4):
                 adds[(n + 1) * ND + at[i]] = (n, i // 2, (0, 1) if i % 2 == 0 else (2, 3))
             finishes[(n + 1) * ND + at[1] + 1] = (n, 0)
             finishes[(n + 1) * ND + at[3] + 1] = (n, 1)
 
-        turn_run(0)
+        norm_at = {}
+        for i in range(14, STEPS):
+            norm_at.setdefault(4 + (i - 14) * (STEPS - AHEAD - 4) // (STEPS - 14), []).append(i)
+        for s in range(4):
+            norm_at[s] = [s + AHEAD]
+
+        gram_at = {2: (6, 7), 4: (8, 9), 6: (10, 11), 8: (12, 13)}
+
+        def grams_of(s):
+            bank = ps_r.tile([P, HALF_B], F32, name="gram", tag="r")
+            for i in gram_at[s]:
+                gram(i, bank)
+
         for s in range(STEPS + LAG):
             n, d = divmod(s, ND)
             new_chunk_due = s < STEPS - AHEAD and s % 4 == 2
-            if new_chunk_due and s > 2:
-                quantise(chunks[(s + AHEAD) // 4])
             if s < STEPS:
                 minus_x_norm(s)
-            if new_chunk_due and s == 2:
-                quantise(chunks[1])
+            if s - 2 in gram_at:
+                for i in gram_at[s - 2]:
+                    diagonal(i)
+            if s - 2 in turned_at and turned_at[s - 2] % 4 == 0:
+                copy_out(runs[turned_at[s - 2]][0], runs[turned_at[s - 2]][1] + 1, False)
+            if s >= LAG and (s - LAG) % ND > 0:
+                running_min(s - LAG, 1 if s < STEPS + LAG - 1 else 2)
+            if new_chunk_due:
+                quantise(chunks[(s + AHEAD) // 4])
             if s + AHEAD < STEPS:
                 mx(s + AHEAD)
+            if s in gram_at:
+                grams_of(s)
             if s in turned_at:
                 turn_run(turned_at[s])
             if s < STEPS:
                 exponential(s, 1 if s < STEPS - 1 else 2)
+                if d == 0:
+                    first_min(n)
+            if s == 0:
+                copy_out(c1, 2, True)
+                copy_out(c1, 3, True)
+                norm_c(1)
             if s - 1 in turned_at:
                 copy_out(runs[turned_at[s - 1]][0], runs[turned_at[s - 1]][1], True)
-            if s in second_at:
-                copy_out(runs[second_at[s]][0], runs[second_at[s]][1] + 1, False)
+                if not (turned_at[s - 1] % 4 == 0):
+                    copy_out(runs[turned_at[s - 1]][0], runs[turned_at[s - 1]][1] + 1, True)
             if s in finishes:
                 finish(finishes[s][0], finishes[s][1])
-            if s + AHEAD < STEPS:
-                norm_c(s + AHEAD)
-            if s >= LAG:
-                running_min(s - LAG, 1 if s < STEPS + 1 else 2)
+            for i in norm_at.get(s, []):
+                norm_c(i)
             if s in adds:
                 add_up(adds[s][0], adds[s][1], adds[s][2])
             if n == LAST and d >= 2:
@@ -337,6 +389,8 @@ def tile_pnn_kernel(tc, x, centers, out):
                 for bh in range(2):
                     last_terms(bh, range(4), (6,), False)
         for bh in range(2):
-            last_terms(bh, range(4), (7,), True)
+            last_terms(bh, range(4), (7,), False)
+        for bh in range(2):
+            last_terms(bh, range(4), (), True)
         finish_last(0)
         finish_last(1)

@@ -213,9 +213,7 @@ def tile_pnn_kernel(tc, x, centers, out):
 
         def first_min(n):
             naccs[n] = small.tile([P, B], F32, name="nacc")
-            nc.gpsimd.tensor_scalar(
-                out=naccs[n][:], in0=e_tiles[n * ND][:], scalar1=-9.0, scalar2=0.0, op0=ALU.mult, op1=ALU.add,
-            )
+            nc.vector.tensor_scalar(out=naccs[n][:], in0=e_tiles[n * ND][:], scalar1=-9.0, scalar2=None, op0=ALU.mult)
 
         def turn(bank_cols, term, cols, first, last):
             nc.tensor.matmul(out=bank_cols, lhsT=term[:, cols], rhs=ident[:], start=first, stop=last, is_transpose=True)
@@ -322,9 +320,9 @@ def tile_pnn_kernel(tc, x, centers, out):
         adds = {}
         finishes = {}
         for n in range(LAST):
-            at = (2, 3, 5, 7) if n < LAST - 1 else (2, 3, 5, 6)
+            at = (2, 2, 6, 6) if n < LAST - 1 else (2, 2, 4, 4)
             for i in range(4):
-                adds[(n + 1) * ND + at[i]] = (n, i // 2, (0, 1) if i % 2 == 0 else (2, 3))
+                adds.setdefault((n + 1) * ND + at[i], []).append((n, i // 2, (0, 1) if i % 2 == 0 else (2, 3)))
             finishes[(n + 1) * ND + at[1] + 1] = (n, 0)
             finishes[(n + 1) * ND + at[3] + 1] = (n, 1)
 
@@ -351,20 +349,25 @@ def tile_pnn_kernel(tc, x, centers, out):
                     diagonal(i)
             if s - 2 in turned_at and turned_at[s - 2] % 4 == 0:
                 copy_out(runs[turned_at[s - 2]][0], runs[turned_at[s - 2]][1] + 1, False)
-            if s >= LAG and (s - LAG) % ND > 0:
+            if s >= LAG and (s - LAG) % ND == 0:
+                first_min((s - LAG) // ND)
+            elif s >= LAG:
                 running_min(s - LAG, 1 if s < STEPS + LAG - 1 else 2)
             if new_chunk_due:
                 quantise(chunks[(s + AHEAD) // 4])
+            if new_chunk_due:
+                for a in adds.get(s, []):
+                    add_up(a[0], a[1], a[2])
+            if new_chunk_due and s in gram_at:
+                grams_of(s)
             if s + AHEAD < STEPS:
                 mx(s + AHEAD)
-            if s in gram_at:
+            if not new_chunk_due and s in gram_at:
                 grams_of(s)
             if s in turned_at:
                 turn_run(turned_at[s])
             if s < STEPS:
                 exponential(s, 1 if s < STEPS - 1 else 2)
-                if d == 0:
-                    first_min(n)
             if s == 0:
                 copy_out(c1, 2, True)
                 copy_out(c1, 3, True)
@@ -377,8 +380,9 @@ def tile_pnn_kernel(tc, x, centers, out):
                 finish(finishes[s][0], finishes[s][1])
             for i in norm_at.get(s, []):
                 norm_c(i)
-            if s in adds:
-                add_up(adds[s][0], adds[s][1], adds[s][2])
+            if not new_chunk_due:
+                for a in adds.get(s, []):
+                    add_up(a[0], a[1], a[2])
             if n == LAST and d >= 2:
                 last_terms(0, (0, 1, 2), (d - 2,), False)
                 if d == 7:

@@ -92,7 +92,7 @@ def tile_pnn_kernel(tc, x, centers, out):
             )
 
         def by_gram(s):
-            return 6 <= s < 14
+            return 6 <= s < 13
 
         grams = {}
 
@@ -327,26 +327,24 @@ def tile_pnn_kernel(tc, x, centers, out):
             finishes[(n + 1) * ND + at[3] + 1] = (n, 1)
 
         norm_at = {}
-        for i in range(14, STEPS):
-            norm_at.setdefault(4 + (i - 14) * (STEPS - AHEAD - 4) // (STEPS - 14), []).append(i)
+        for i in range(13, STEPS):
+            norm_at.setdefault(4 + (i - 13) * (STEPS - AHEAD - 4) // (STEPS - 13), []).append(i)
         for s in range(4):
             norm_at[s] = [s + AHEAD]
 
-        gram_at = {2: (6, 7), 4: (8, 9), 6: (10, 11), 8: (12, 13)}
+        gram_at = {i - 4: i for i in range(6, 13)}
 
         def grams_of(s):
             bank = ps_r.tile([P, HALF_B], F32, name="gram", tag="r")
-            for i in gram_at[s]:
-                gram(i, bank)
+            gram(gram_at[s], bank)
 
         for s in range(STEPS + LAG):
             n, d = divmod(s, ND)
             new_chunk_due = s < STEPS - AHEAD and s % 4 == 2
             if s < STEPS:
                 minus_x_norm(s)
-            if s - 2 in gram_at:
-                for i in gram_at[s - 2]:
-                    diagonal(i)
+            if s - 1 in gram_at:
+                diagonal(gram_at[s - 1])
             if s - 2 in turned_at and turned_at[s - 2] % 4 == 0:
                 copy_out(runs[turned_at[s - 2]][0], runs[turned_at[s - 2]][1] + 1, False)
             if s >= LAG and (s - LAG) % ND == 0:

@@ -343,14 +343,14 @@ def tile_pnn_kernel(tc, x, centers, out):
             new_chunk_due = s < STEPS - AHEAD and s % 4 == 2
             if s < STEPS:
                 minus_x_norm(s)
-            if s - 1 in gram_at:
-                diagonal(gram_at[s - 1])
-            if s - 2 in turned_at and turned_at[s - 2] % 4 == 0:
+            if s - 2 in turned_at and turned_at[s - 2] % 3 == 0:
                 copy_out(runs[turned_at[s - 2]][0], runs[turned_at[s - 2]][1] + 1, False)
             if s >= LAG and (s - LAG) % ND == 0:
                 first_min((s - LAG) // ND)
             elif s >= LAG:
                 running_min(s - LAG, 1 if s < STEPS + LAG - 1 else 2)
+            if s - 1 in gram_at:
+                diagonal(gram_at[s - 1])
             if new_chunk_due:
                 quantise(chunks[(s + AHEAD) // 4])
             if new_chunk_due:
@@ -372,7 +372,7 @@ def tile_pnn_kernel(tc, x, centers, out):
                 norm_c(1)
             if s - 1 in turned_at:
                 copy_out(runs[turned_at[s - 1]][0], runs[turned_at[s - 1]][1], True)
-                if not (turned_at[s - 1] % 4 == 0):
+                if not (turned_at[s - 1] % 3 == 0):
                     copy_out(runs[turned_at[s - 1]][0], runs[turned_at[s - 1]][1] + 1, True)
             if s in finishes:
                 finish(finishes[s][0], finishes[s][1])

@@ -43,6 +43,8 @@ def tile_pnn_kernel(tc, x, centers, out):
         warm = const.tile([P, 1], F32, name="warm")
         nc.vector.memset(warm[:], 0.0)
         nc.scalar.activation(out=warm[:], in_=warm[:], func=ACT.Exp)
+        zeros = const.tile([P, P + HALF_B], BF16, name="zeros")
+        nc.vector.memset(zeros[:], 0.0)
         ident = const.tile([P, P], F32, name="ident")
         make_identity(nc, ident[:])
         junk_s = const.tile([P, FEAT], BF16, name="junk_s")
@@ -274,13 +276,23 @@ def tile_pnn_kernel(tc, x, centers, out):
         ctx.enter_context(tc.manual_schedule(engines={mybir.EngineType.PE, mybir.EngineType.DVE, mybir.EngineType.Activation}))
         c0 = cs[(0, 0)]
 
+        dummy = ps_g.tile([P, HALF_B], F32, name="g")
+
+        def keep_warm():
+            nc.tensor.matmul(out=dummy[:], lhsT=zeros[:, 0:P], rhs=zeros[:, P:], start=True, stop=True)
+
+        for i in range(4):
+            keep_warm()
+
         c1 = cs[(0, 1)]
         for j in range(4):
             transposes(xs[0], j)
+            keep_warm()
             norm(xs[0], j)
             copy_out(xs[0], j, False)
         for j in range(4):
             transposes(xs[1], j)
+            keep_warm()
             norm(xs[1], j)
             copy_out(xs[1], j, False)
             if j == 0:
@@ -290,6 +302,7 @@ def tile_pnn_kernel(tc, x, centers, out):
                 copy_x_norm(0)
         for j in range(2):
             transposes(c0, j)
+            keep_warm()
             copy_out(c0, j, False)
         quantise(xs[1])
         quantise(c0, 0, 2)
@@ -391,8 +404,5 @@ def tile_pnn_kernel(tc, x, centers, out):
                 for bh in range(2):
                     last_terms(bh, range(4), (6,), False)
         for bh in range(2):
-            last_terms(bh, range(4), (7,), False)
-        for bh in range(2):
-            last_terms(bh, range(4), (), True)
-        finish_last(0)
-        finish_last(1)
+            last_terms(bh, range(4), (7,), True)
+            finish_last(bh)

@@ -93,8 +93,12 @@ def tile_pnn_kernel(tc, x, centers, out):
                 out=junk_s[:], in_=blk, func=ACT.Square, scale=math.sqrt(0.5), accum_out=chunk["half"][:, j : j + 1],
             )
 
+        gram_at = {i - 4: i for i in range(6, 13)}
+        gram_at.update({12: 16})
+        gram_steps = set(gram_at.values())
+
         def by_gram(s):
-            return 6 <= s < 13
+            return s in gram_steps
 
         grams = {}
 
@@ -233,10 +237,11 @@ def tile_pnn_kernel(tc, x, centers, out):
                         i == 0, i == len(terms) - 1,
                     )
 
-        def store(n, bh, res):
+        def store(n, bh, res, first=0, count=4):
+            ts = slice(first, first + count)
             nc.sync.dma_start(
-                out=out[bh * HALF_B : (bh + 1) * HALF_B, n * P : (n + 1) * P].rearrange("(p t) o -> p t o", t=4),
-                in_=res[:].rearrange("p (t o) -> p t o", t=4),
+                out=out[bh * HALF_B : (bh + 1) * HALF_B, n * P : (n + 1) * P].rearrange("(p t) o -> p t o", t=4)[:, ts, :],
+                in_=res[:].rearrange("p (t o) -> p t o", t=4)[:, ts, :],
             )
 
         def finish(n, bh):
@@ -271,7 +276,8 @@ def tile_pnn_kernel(tc, x, centers, out):
                     nc.scalar.mul(out=dst, in_=last_banks[(bh, t)][:, 0:P], mul=-0.125)
                 else:
                     nc.vector.tensor_scalar(out=dst, in0=last_banks[(bh, t)][:, 0:P], scalar1=-0.125, scalar2=None, op0=ALU.mult)
-            store(LAST, bh, res)
+                if t % 2 == 1:
+                    store(LAST, bh, res, t - 1, 2)
 
         ctx.enter_context(tc.manual_schedule(engines={mybir.EngineType.PE, mybir.EngineType.DVE, mybir.EngineType.Activation}))
         c0 = cs[(0, 0)]
@@ -339,13 +345,10 @@ def tile_pnn_kernel(tc, x, centers, out):
             finishes[(n + 1) * ND + at[1] + 1] = (n, 0)
             finishes[(n + 1) * ND + at[3] + 1] = (n, 1)
 
-        norm_at = {}
-        for i in range(13, STEPS):
-            norm_at.setdefault(4 + (i - 13) * (STEPS - AHEAD - 4) // (STEPS - 13), []).append(i)
-        for s in range(4):
-            norm_at[s] = [s + AHEAD]
-
-        gram_at = {i - 4: i for i in range(6, 13)}
+        norm_at = {s: [s + AHEAD] for s in range(4)}
+        rest = [i for i in range(6, STEPS) if not by_gram(i)]
+        for k, i in enumerate(rest):
+            norm_at.setdefault(4 + k * (STEPS - AHEAD - 4) // len(rest), []).append(i)
 
         def grams_of(s):
             bank = ps_r.tile([P, HALF_B], F32, name="gram", tag="r")
@@ -356,7 +359,7 @@ def tile_pnn_kernel(tc, x, centers, out):
             new_chunk_due = s < STEPS - AHEAD and s % 4 == 2
             if s < STEPS:
                 minus_x_norm(s)
-            if s - 2 in turned_at and turned_at[s - 2] % 3 == 0:
+            if s - 2 in turned_at and turned_at[s - 2] % 4 == 0:
                 copy_out(runs[turned_at[s - 2]][0], runs[turned_at[s - 2]][1] + 1, False)
             if s >= LAG and (s - LAG) % ND == 0:
                 first_min((s - LAG) // ND)
@@ -385,7 +388,7 @@ def tile_pnn_kernel(tc, x, centers, out):
                 norm_c(1)
             if s - 1 in turned_at:
                 copy_out(runs[turned_at[s - 1]][0], runs[turned_at[s - 1]][1], True)
-                if not (turned_at[s - 1] % 3 == 0):
+                if not (turned_at[s - 1] % 4 == 0):
                     copy_out(runs[turned_at[s - 1]][0], runs[turned_at[s - 1]][1] + 1, True)
             if s in finishes:
                 finish(finishes[s][0], finishes[s][1])

@@ -43,7 +43,7 @@ def tile_pnn_kernel(tc, x, centers, out):
         warm = const.tile([P, 1], F32, name="warm")
         nc.vector.memset(warm[:], 0.0)
         nc.scalar.activation(out=warm[:], in_=warm[:], func=ACT.Exp)
-        zeros = const.tile([P, P + HALF_B], BF16, name="zeros")
+        zeros = const.tile([P, HALF_B], BF16, name="zeros")
         nc.vector.memset(zeros[:], 0.0)
         ident = const.tile([P, P], F32, name="ident")
         make_identity(nc, ident[:])
@@ -285,9 +285,9 @@ def tile_pnn_kernel(tc, x, centers, out):
         dummy = ps_g.tile([P, HALF_B], F32, name="g")
 
         def keep_warm():
-            nc.tensor.matmul(out=dummy[:], lhsT=zeros[:, 0:P], rhs=zeros[:, P:], start=True, stop=True)
+            nc.tensor.matmul(out=dummy[:], lhsT=zeros[:, 0:P], rhs=zeros[:], start=True, stop=True)
 
-        for i in range(4):
+        for i in range(3):
             keep_warm()
 
         c1 = cs[(0, 1)]

import math
from contextlib import ExitStack

import concourse.mybir as mybir
from concourse.masks import make_identity

F32 = mybir.dt.float32
BF16 = mybir.dt.bfloat16
U32 = mybir.dt.uint32
U8 = mybir.dt.uint8
FP8X4 = mybir.dt.float8_e4m3fn_x4
ALU = mybir.AluOpType
ACT = mybir.ActivationFunctionType

P = 128
FEAT = 1024
WORDS = FEAT // 2
B = 1024
ND = 8
TILES = 4
HALF_B = 512
STEPS = TILES * ND
LAST = TILES - 1
AHEAD = 2
LAG = 2

FLOPS = 2 * 1024 * 4096 * 1024


def tile_pnn_kernel(tc, x, centers, out):
    nc = tc.nc
    with ExitStack() as ctx:
        const = ctx.enter_context(tc.tile_pool(name="const", bufs=1))
        nat = ctx.enter_context(tc.tile_pool(name="nat", bufs=8))
        keep = ctx.enter_context(tc.tile_pool(name="keep", bufs=1))
        stage = ctx.enter_context(tc.tile_pool(name="stage", bufs=3))
        probs = ctx.enter_context(tc.tile_pool(name="probs", bufs=18))
        small = ctx.enter_context(tc.tile_pool(name="small", bufs=2))
        ps_g = ctx.enter_context(tc.psum_pool(name="ps_g", bufs=4))
        ps_t = ctx.enter_context(tc.psum_pool(name="ps_t", bufs=3))
        ps_r = ctx.enter_context(tc.psum_pool(name="ps_r", bufs=1))

        warm = const.tile([P, 1], F32, name="warm")
        nc.vector.memset(warm[:], 0.0)
        nc.scalar.activation(out=warm[:], in_=warm[:], func=ACT.Exp)
        zeros = const.tile([P, HALF_B], BF16, name="zeros")
        nc.vector.memset(zeros[:], 0.0)
        ident = const.tile([P, P], F32, name="ident")
        make_identity(nc, ident[:])
        junk_s = const.tile([P, FEAT], BF16, name="junk_s")
        junk_v = const.tile([P, P], F32, name="junk_v")
        xb = const.tile([P, B], F32, name="xb")

        def new_chunk(kind, a, b):
            tagname = "%s%d%d" % (kind, a, b)
            return {
                "kind": kind,
                "nat": nat.tile([P, 4 * FEAT], BF16, name="nat_" + tagname, tag="nat"),
                "codes": keep.tile([P, 4 * FEAT // 4], U32, name="codes_" + tagname, align_bytes=64),
                "scales": keep.tile([P, 4 * FEAT // 4], U8, name="scales_" + tagname, align_bytes=64),
                "half": keep.tile([P, 4], F32, name="half_" + tagname),
                "neg": keep.tile([P, 4], F32, name="neg_" + tagname),
                "neg_v": keep.tile([P, 4], F32, name="negv_" + tagname),
                "banks": {},
            }

        def load(chunk, src, pieces):
            dst = chunk["nat"][:].rearrange("p (t k) -> p t k", t=4)
            step = 4 // pieces
            for i in range(pieces):
                nc.sync.dma_start(out=dst[:, i * step : (i + 1) * step, :], in_=src[:, i * step : (i + 1) * step, :])

        xs = {}
        cs = {}

        def load_x(bh, pieces):
            xs[bh] = new_chunk("x", bh, 0)
            load(xs[bh], x[bh * HALF_B : (bh + 1) * HALF_B, :].rearrange("(p t) k -> p t k", t=4), pieces)

        def load_c(ot, h, pieces):
            cs[(ot, h)] = new_chunk("c", ot, h)
            load(cs[(ot, h)], centers[ot * P : (ot + 1) * P, 4 * h : 4 * h + 4, :], pieces)

        load_x(0, 4)
        load_x(1, 2)
        for ot in range(TILES):
            for h in range(2):
                load_c(ot, h, 1)

        def norm(chunk, j):
            blk = chunk["nat"][:, j * FEAT : (j + 1) * FEAT]
            nc.scalar.activation(
                out=junk_s[:], in_=blk, func=ACT.Square, scale=math.sqrt(0.5), accum_out=chunk["half"][:, j : j + 1],
            )

        gram_at = {i - 4: i for i in range(6, 13)}
        gram_at.update({12: 16})
        gram_steps = set(gram_at.values())

        def by_gram(s):
            return s in gram_steps

        grams = {}

        def gram(s, bank):
            chunk = cs[(s // ND, s % ND // 4)]
            out_cols = bank[:, s % 4 * P : (s % 4 + 1) * P]
            rows = chunk["grouped"][:, (s % 4) * FEAT : (s % 4 + 1) * FEAT].rearrange("p (g r k) -> p g k r", g=2, k=4)
            for i in range(8):
                v = rows[:, i // 4, i % 4, :]
                nc.tensor.matmul(out=out_cols, lhsT=v, rhs=v, start=(i == 0), stop=(i == 7))
            grams[s] = out_cols

        def diagonal(s):
            chunk = cs[(s // ND, s % ND // 4)]
            nc.vector.scalar_tensor_tensor(
                out=junk_v[:], in0=grams[s], scalar=-0.5, in1=ident[:], op0=ALU.mult, op1=ALU.mult,
                accum_out=chunk["neg_v"][:, s % 4 : s % 4 + 1],
            )

        def norm_c(s):
            ot, d = divmod(s, ND)
            chunk = cs[(ot, d // 4)]
            j = d % 4
            norm(chunk, j)
            nc.gpsimd.tensor_scalar(
                out=chunk["neg"][:, j : j + 1], in0=chunk["half"][:, j : j + 1], scalar1=-1.0, scalar2=0.0,
                op0=ALU.mult, op1=ALU.add,
            )

        def transposes(chunk, j):
            bank = ps_t.tile([P, WORDS], F32, name="xt")
            words = chunk["nat"][:].bitcast(F32)
            for q in range(4):
                nc.tensor.transpose(
                    bank[:, q * P : (q + 1) * P],
                    words[:, j * WORDS + q * P : j * WORDS + (q + 1) * P],
                    ident[:],
                )
            chunk["banks"][j] = bank

        def copy_out(chunk, j, on_scalar):
            if j == 0:
                chunk["grouped"] = stage.tile([P, 4 * FEAT], BF16, name="grouped", align_bytes=64)
            gw = chunk["grouped"][:].bitcast(F32)
            src = chunk["banks"][j][:].rearrange("p (g u r) -> p g r u", g=2, u=2)
            if chunk["kind"] == "c":
                dst = gw[:, j * WORDS : (j + 1) * WORDS].rearrange("p (g r u) -> p g r u", g=2, u=2)
            else:
                dst = gw.rearrange("p (g c u) -> p g c u", g=2, u=2)[:, :, j * P : (j + 1) * P, :]
            if on_scalar:
                nc.scalar.copy(out=dst, in_=src)
            else:
                nc.vector.tensor_copy(out=dst, in_=src)

        def quantise(chunk, part=0, parts=1):
            w = slice(part * FEAT // parts, (part + 1) * FEAT // parts)
            nc.vector.quantize_mx(
                out=chunk["codes"][:, w].bitcast(FP8X4), scales=chunk["scales"][:, w],
                in_=chunk["grouped"][:, 4 * w.start : 4 * w.stop],
            )

        def spread_x_norm(bh):
            bank = ps_r.tile([P, HALF_B], F32, name="xrow", tag="r")
            for t in range(4):
                nc.tensor.matmul(
                    out=bank[:, t * P : (t + 1) * P],
                    lhsT=xs[bh]["half"][:, t : t + 1].to_broadcast([P, P]),
                    rhs=ident[:], start=True, stop=True,
                )
            xs[bh]["row"] = bank

        def copy_x_norm(bh):
            nc.scalar.copy(out=xb[:, bh * HALF_B : (bh + 1) * HALF_B], in_=xs[bh]["row"][:])

        g_banks = {}
        e_tiles = {}
        naccs = {}

        def mx(s):
            ot, d = divmod(s, ND)
            c = cs[(ot, d // 4)]
            for bh in range(2):
                bank = ps_g.tile([P, HALF_B], F32, name="g")
                for g in range(2):
                    w = slice((d % 4) * 2 * P + g * P, (d % 4) * 2 * P + (g + 1) * P)
                    m = slice(g * HALF_B, (g + 1) * HALF_B)
                    nc.tensor.matmul_mx(
                        out=bank[:],
                        lhsT=c["codes"][:, w].bitcast(FP8X4), lhsT_scale=c["scales"][:, w],
                        rhs=xs[bh]["codes"][:, m].bitcast(FP8X4), rhs_scale=xs[bh]["scales"][:, m],
                        start=(g == 0), stop=(g == 1),
                    )
                g_banks[(s, bh)] = bank

        def minus_x_norm(s):
            e = probs.tile([P, B], F32, name="e")
            for bh in range(2):
                w = slice(bh * HALF_B, (bh + 1) * HALF_B)
                nc.vector.tensor_tensor(out=e[:, w], in0=g_banks[(s, bh)][:], in1=xb[:, w], op=ALU.subtract)
            e_tiles[s] = e

        def exponential(s, widths):
            ot, d = divmod(s, ND)
            e = e_tiles[s]
            for i in range(widths):
                w = slice(i * B // widths, (i + 1) * B // widths)
                nc.scalar.activation(
                    out=e[:, w], in_=e[:, w], func=ACT.Exp, bias=cs[(ot, d // 4)]["neg_v" if by_gram(s) else "neg"][:, d % 4 : d % 4 + 1],
                )

        def running_min(s, widths):
            n, d = divmod(s, ND)
            for i in range(widths):
                w = slice(i * B // widths, (i + 1) * B // widths)
                nc.vector.scalar_tensor_tensor(
                    out=naccs[n][:, w], in0=e_tiles[s][:, w], scalar=-9.0, in1=naccs[n][:, w], op0=ALU.mult, op1=ALU.min,
                )

        def first_min(n):
            naccs[n] = small.tile([P, B], F32, name="nacc")
            nc.vector.tensor_scalar(out=naccs[n][:], in0=e_tiles[n * ND][:], scalar1=-9.0, scalar2=None, op0=ALU.mult)

        def turn(bank_cols, term, cols, first, last):
            nc.tensor.matmul(out=bank_cols, lhsT=term[:, cols], rhs=ident[:], start=first, stop=last, is_transpose=True)

        r_banks = {}

        def add_up(n, bh, blocks):
            if blocks[0] == 0:
                r_banks[(n, bh)] = ps_r.tile([P, HALF_B], F32, name="r", tag="r")
            terms = [e_tiles[n * ND + d] for d in range(ND)] + [naccs[n]]
            for t in blocks:
                for i, term in enumerate(terms):
                    turn(
                        r_banks[(n, bh)][:, t * P : (t + 1) * P], term, slice(bh * HALF_B + t * P, bh * HALF_B + (t + 1) * P),
                        i == 0, i == len(terms) - 1,
                    )

        def store(n, bh, res, first=0, count=4):
            ts = slice(first, first + count)
            nc.sync.dma_start(
                out=out[bh * HALF_B : (bh + 1) * HALF_B, n * P : (n + 1) * P].rearrange("(p t) o -> p t o", t=4)[:, ts, :],
                in_=res[:].rearrange("p (t o) -> p t o", t=4)[:, ts, :],
            )

        def finish(n, bh):
            res = small.tile([P, HALF_B], F32, name="res")
            nc.scalar.mul(out=res[:], in_=r_banks[(n, bh)][:], mul=-0.125)
            store(n, bh, res)

        last_banks = {}

        def last_terms(bh, blocks, ds, with_max):
            for t in blocks:
                if (bh, t) not in last_banks:
                    if bh == 0 and t < 3:
                        last_banks[(bh, t)] = ps_t.tile([P, WORDS], F32, name="xt")
                    elif bh == 0:
                        last_banks[(bh, t)] = ps_r.tile([P, HALF_B], F32, name="r", tag="r")
                    else:
                        last_banks[(bh, t)] = ps_g.tile([P, HALF_B], F32, name="g")
            for i in list(ds) + ([ND] if with_max else []):
                for t in blocks:
                    term = naccs[LAST] if i == ND else e_tiles[LAST * ND + i]
                    turn(
                        last_banks[(bh, t)][:, 0:P], term, slice(bh * HALF_B + t * P, bh * HALF_B + (t + 1) * P),
                        i == 0, i == ND,
                    )

        def finish_last(bh):
            res = small.tile([P, HALF_B], F32, name="res")
            for t in range(4):
                dst = res[:, t * P : (t + 1) * P]
                if t % 2 == 0:
                    nc.scalar.mul(out=dst, in_=last_banks[(bh, t)][:, 0:P], mul=-0.125)
                else:
                    nc.vector.tensor_scalar(out=dst, in0=last_banks[(bh, t)][:, 0:P], scalar1=-0.125, scalar2=None, op0=ALU.mult)
                if t % 2 == 1:
                    store(LAST, bh, res, t - 1, 2)

        ctx.enter_context(tc.manual_schedule(engines={mybir.EngineType.PE, mybir.EngineType.DVE, mybir.EngineType.Activation}))
        c0 = cs[(0, 0)]

        dummy = ps_g.tile([P, HALF_B], F32, name="g")

        def keep_warm():
            nc.tensor.matmul(out=dummy[:], lhsT=zeros[:, 0:P], rhs=zeros[:], start=True, stop=True)

        for i in range(3):
            keep_warm()

        c1 = cs[(0, 1)]
        for j in range(4):
            transposes(xs[0], j)
            keep_warm()
            norm(xs[0], j)
            copy_out(xs[0], j, False)
        for j in range(4):
            transposes(xs[1], j)
            keep_warm()
            norm(xs[1], j)
            copy_out(xs[1], j, False)
            if j == 0:
                quantise(xs[0])
            if j == 2:
                spread_x_norm(0)
                copy_x_norm(0)
        for j in range(2):
            transposes(c0, j)
            keep_warm()
            copy_out(c0, j, False)
        quantise(xs[1])
        quantise(c0, 0, 2)
        for j in range(2, 4):
            transposes(c0, j)
            copy_out(c0, j, False)
        transposes(c1, 0)
        spread_x_norm(1)
        norm_c(0)
        copy_x_norm(1)
        copy_out(c1, 0, True)
        mx(0)
        transposes(c1, 1)
        copy_out(c1, 1, True)
        mx(1)
        quantise(c0, 1, 2)
        transposes(c1, 2)
        transposes(c1, 3)

        chunks = [cs[(k // 2, k % 2)] for k in range(2 * TILES)]
        runs = [(chunks[k], j) for k in range(2, 2 * TILES) for j in (0, 2)]
        turned_at = {2 * r + 1: r for r in range(len(runs))}

        def turn_run(r):
            for j in range(2):
                transposes(runs[r][0], runs[r][1] + j)

        adds = {}
        finishes = {}
        for n in range(LAST):
            at = (2, 2, 6, 6) if n < LAST - 1 else (2, 2, 4, 4)
            for i in range(4):
                adds.setdefault((n + 1) * ND + at[i], []).append((n, i // 2, (0, 1) if i % 2 == 0 else (2, 3)))
            finishes[(n + 1) * ND + at[1] + 1] = (n, 0)
            finishes[(n + 1) * ND + at[3] + 1] = (n, 1)

        norm_at = {s: [s + AHEAD] for s in range(4)}
        rest = [i for i in range(6, STEPS) if not by_gram(i)]
        for k, i in enumerate(rest):
            norm_at.setdefault(4 + k * (STEPS - AHEAD - 4) // len(rest), []).append(i)

        def grams_of(s):
            bank = ps_r.tile([P, HALF_B], F32, name="gram", tag="r")
            gram(gram_at[s], bank)

        for s in range(STEPS + LAG):
            n, d = divmod(s, ND)
            new_chunk_due = s < STEPS - AHEAD and s % 4 == 2
            if s < STEPS:
                minus_x_norm(s)
            if s - 2 in turned_at and turned_at[s - 2] % 4 == 0:
                copy_out(runs[turned_at[s - 2]][0], runs[turned_at[s - 2]][1] + 1, False)
            if s >= LAG and (s - LAG) % ND == 0:
                first_min((s - LAG) // ND)
            elif s >= LAG:
                running_min(s - LAG, 1 if s < STEPS + LAG - 1 else 2)
            if s - 1 in gram_at:
                diagonal(gram_at[s - 1])
            if new_chunk_due:
                quantise(chunks[(s + AHEAD) // 4])
            if new_chunk_due:
                for a in adds.get(s, []):
                    add_up(a[0], a[1], a[2])
            if new_chunk_due and s in gram_at:
                grams_of(s)
            if s + AHEAD < STEPS:
                mx(s + AHEAD)
            if not new_chunk_due and s in gram_at:
                grams_of(s)
            if s in turned_at:
                turn_run(turned_at[s])
            if s < STEPS:
                exponential(s, 1 if s < STEPS - 1 else 2)
            if s == 0:
                copy_out(c1, 2, True)
                copy_out(c1, 3, True)
                norm_c(1)
            if s - 1 in turned_at:
                copy_out(runs[turned_at[s - 1]][0], runs[turned_at[s - 1]][1], True)
                if not (turned_at[s - 1] % 4 == 0):
                    copy_out(runs[turned_at[s - 1]][0], runs[turned_at[s - 1]][1] + 1, True)
            if s in finishes:
                finish(finishes[s][0], finishes[s][1])
            for i in norm_at.get(s, []):
                norm_c(i)
            if not new_chunk_due:
                for a in adds.get(s, []):
                    add_up(a[0], a[1], a[2])
            if n == LAST and d >= 2:
                last_terms(0, (0, 1, 2), (d - 2,), False)
                if d == 7:
                    last_terms(1, (0, 1), range(0, 6), False)
            if s == STEPS:
                last_terms(0, (3,), range(0, 6), False)
                last_terms(1, (2, 3), range(0, 6), False)
                for bh in range(2):
                    last_terms(bh, range(4), (6,), False)
        for bh in range(2):
            last_terms(bh, range(4), (7,), True)
            finish_last(bh)
